import numpy as np
import ml_dtypes


def mxq(x, axis, fmt="e4m3"):
    dtype, down = {"e4m3": (ml_dtypes.float8_e4m3fn, 7), "e5m2": (ml_dtypes.float8_e5m2, 14)}[fmt]
    v = np.moveaxis(np.asarray(x, np.float32).astype(ml_dtypes.bfloat16).astype(np.float64), axis, -1)
    blocks = v.reshape(v.shape[:-1] + (-1, 32))
    amax = np.abs(blocks).max(-1, keepdims=True)
    byte = np.maximum(np.where(amax > 0, np.frexp(amax)[1] - 1 + 127, 0) - down, 1)
    scale = np.exp2(byte - 127.0)
    codes = (blocks / scale).astype(np.float32).astype(dtype).astype(np.float64)
    return np.moveaxis((codes * scale).reshape(v.shape), -1, axis)


WIDE = False


def mx_kscale(k):
    if not WIDE:
        return np.ones(k)
    levels = np.array([10, -10, 5, -5, 0])
    a = np.random.permutation(np.resize(levels, k // 512 * 4)).reshape(k // 512, 4)
    idx = np.arange(k)
    return np.exp2(a[idx // 512, idx % 128 // 32])


BF16 = ml_dtypes.bfloat16


def bf(x):
    return np.asarray(x, np.float32).astype(BF16)


def f64(x):
    return np.asarray(x).astype(np.float64)


B, T, D, H = 128, 32, 1024, 1
NEG_INF = -1e30


def setup_inputs():
    s = mx_kscale(D)
    return {"h": bf(np.random.standard_normal((B, T, D)) * s),
            "A": bf(np.random.standard_normal((H, D, D)) * 3.0 / D / s[:, None] / s[None, :])}


def reference(h, A):
    hq = mxq(f64(h), 2, "e4m3")
    hA = hq[:, None, 1:] @ mxq(f64(A), 1, "e4m3")[None]
    rest = mxq(hA, 3, "e4m3") @ hq[:, None].transpose(0, 1, 3, 2)
    scores = np.concatenate([np.zeros((B, H, 1, T)), rest], axis=2)
    causal = np.tril(np.ones((T, T), dtype=bool))
    scores = np.where(causal, scores, NEG_INF)
    e = np.exp(scores - scores.max(-1, keepdims=True))
    return e / e.sum(-1, keepdims=True)

@@ -1,0 +1,268 @@
+from contextlib import ExitStack
+
+import concourse.mybir as mybir
+from concourse.masks import make_identity
+
+F32 = mybir.dt.float32
+BF16 = mybir.dt.bfloat16
+U32 = mybir.dt.uint32
+U8 = mybir.dt.uint8
+FP8X4 = mybir.dt.float8_e4m3fn_x4
+ALU = mybir.AluOpType
+ACT = mybir.ActivationFunctionType
+AXIS = mybir.AxisListType
+
+P = 128
+SEQS, T, D = 128, 32, 1024
+PACK = 4
+K_PASS = P * PACK
+PASSES = D // K_PASS
+GROUPS = SEQS * T // P
+SEQS_IN_GROUP = P // T
+ROUND = 4
+ROUNDS = GROUPS // ROUND
+WORDS = D // 2
+NEG_INF = -1e30
+
+FLOPS = 2 * SEQS * (T - 1) * D * D + 2 * SEQS * (T - 1) * D * T
+
+
+def tile_causalselfattention_pa_t_kernel(tc, h, A, out):
+    nc = tc.nc
+    with ExitStack() as ctx:
+        keep = ctx.enter_context(tc.tile_pool(name="keep", bufs=1))
+        h_stage = ctx.enter_context(tc.tile_pool(name="h_stage", bufs=2 * ROUND))
+        ha_stage = ctx.enter_context(tc.tile_pool(name="ha_stage", bufs=ROUND))
+        soft = ctx.enter_context(tc.tile_pool(name="soft", bufs=2))
+        xt_psum = ctx.enter_context(tc.psum_pool(name="xt_psum", bufs=ROUND))
+        ha_psum = ctx.enter_context(tc.psum_pool(name="ha_psum", bufs=3))
+        score_psum = ctx.enter_context(tc.psum_pool(name="score_psum", bufs=1))
+
+        identity = keep.tile([P, P], F32)
+        make_identity(nc, identity[:])
+        mask = keep.tile([P, P], F32)
+        nc.gpsimd.memset(mask[:], 0.0)
+        nc.gpsimd.affine_select(
+            out=mask[:],
+            in_=mask[:],
+            pattern=[[-1, P]],
+            compare_op=ALU.is_ge,
+            fill=NEG_INF,
+            base=0,
+            channel_multiplier=1,
+        )
+        table_in = keep.tile([P, 1], F32)
+        table_out = keep.tile([P, 1], F32)
+        nc.vector.memset(table_in[:], 0.0)
+        nc.scalar.activation(out=table_out[:], in_=table_in[:], func=ACT.Exp)
+
+        h_raw = keep.tile([P, GROUPS, D], BF16)
+        h_words = h_raw[:].rearrange("p g d -> p (g d)").bitcast(F32)
+        h_codes = keep.tile([P, GROUPS, PASSES * P], U32, align_bytes=64)
+        h_scales = keep.tile([P, GROUPS, PASSES * P], U8, align_bytes=64)
+        a_raw = keep.tile([P, PASSES, PACK, D], BF16)
+        a_codes = keep.tile([P, PASSES, D], U32, align_bytes=64)
+        a_scales = keep.tile([P, PASSES, D], U8, align_bytes=64)
+        ha_codes = keep.tile([P, GROUPS, PASSES * P], U32, align_bytes=64)
+        ha_scales = keep.tile([P, GROUPS, PASSES * P], U8, align_bytes=64)
+        attn = keep.tile([P, GROUPS, T], F32)
+
+        h_rows = h.rearrange("b t d -> (b t) d").rearrange("(g p) d -> p g d", p=P)
+        a_rows = A.rearrange("n (c u p v) e -> p (n c) u (v e)", c=PASSES, u=2, v=2)
+        out_rows = out.rearrange("(g b) n t s -> (b n t) g s", b=SEQS_IN_GROUP)
+
+        def load_h(first, last):
+            nc.sync.dma_start(out=h_raw[:, first:last, :], in_=h_rows[:, first:last, :])
+
+        load_h(0, 1)
+        for dp in range(PASSES):
+            nc.sync.dma_start(
+                out=a_raw[:, dp].rearrange("p (u v) e -> p u (v e)", u=2), in_=a_rows[:, dp]
+            )
+        load_h(1, ROUND)
+        for r in range(1, ROUNDS):
+            load_h(r * ROUND, (r + 1) * ROUND)
+
+        xt_banks = {}
+        h_grouped = {}
+        ha_grouped = {}
+        score_banks = {}
+        exps = {}
+
+        def transpose_round(r):
+            for grp in range(r * ROUND, (r + 1) * ROUND):
+                xt_banks[grp] = xt_psum.tile([P, PACK, P], F32, name="xt_bank")
+                for quarter in range(PACK):
+                    first_word = grp * WORDS + quarter * P
+                    nc.tensor.transpose(
+                        xt_banks[grp][:, quarter, :],
+                        h_words[:, first_word : first_word + P],
+                        identity[:],
+                    )
+
+        def copy_h(grp):
+            h_grouped[grp] = h_stage.tile([P, PASSES * P * PACK], BF16, align_bytes=64, name="h_grouped")
+            pairs_out = h_grouped[grp][:].bitcast(F32).rearrange("p (c r u) -> p c r u", c=PASSES, u=2)
+            pairs_in = xt_banks[grp][:].rearrange("p (c u) r -> p c r u", u=2)
+            if grp % ROUND == 0:
+                nc.scalar.copy(out=pairs_out, in_=pairs_in)
+            else:
+                nc.vector.tensor_copy(out=pairs_out, in_=pairs_in)
+
+        def quantise_h(grp):
+            nc.vector.quantize_mx(
+                out=h_codes[:, grp, :].bitcast(FP8X4),
+                scales=h_scales[:, grp, :],
+                in_=h_grouped[grp][:],
+            )
+
+        def quantise_a():
+            pieces = [(dp, ep) for dp in range(PASSES) for ep in range(PASSES)]
+            grouped = {}
+
+            def quantise_piece(dp, ep):
+                places = slice(ep * K_PASS, (ep + 1) * K_PASS)
+                nc.vector.quantize_mx(
+                    out=a_codes[:, dp, places].bitcast(FP8X4),
+                    scales=a_scales[:, dp, places],
+                    in_=grouped[dp, ep][:].rearrange("p u v q j -> p (u v q j)"),
+                )
+
+            for i, (dp, ep) in enumerate(pieces):
+                grouped[dp, ep] = keep.tile(
+                    [P, 2, 2, P, PACK], BF16, align_bytes=64, name="a_grouped%d%d" % (dp, ep)
+                )
+                for u in range(2):
+                    first_col = ep * K_PASS + u * 2 * P
+                    src = a_raw[:, dp, :, first_col : first_col + 2 * P]
+                    src = src.rearrange("p j (q v) -> p v q j", v=2)
+                    if u == 0:
+                        nc.vector.tensor_copy(out=grouped[dp, ep][:, u], in_=src)
+                    else:
+                        nc.scalar.copy(out=grouped[dp, ep][:, u], in_=src)
+                if i > 0:
+                    quantise_piece(*pieces[i - 1])
+            quantise_piece(*pieces[-1])
+
+        def first_matmul(grp):
+            ha_grouped[grp] = ha_stage.tile([P, PASSES, P, PACK], BF16, align_bytes=64, name="ha_grouped")
+            for ep in range(PASSES):
+                ha_bank = ha_psum.tile([P, PACK, P], F32)
+                for slot in range(PACK):
+                    places = slice((ep * PACK + slot) * P, (ep * PACK + slot + 1) * P)
+                    for dp in range(PASSES):
+                        tokens = slice(dp * P, (dp + 1) * P)
+                        nc.tensor.matmul_mx(
+                            out=ha_bank[:, slot, :],
+                            lhsT=a_codes[:, dp, places].bitcast(FP8X4),
+                            lhsT_scale=a_scales[:, dp, places],
+                            rhs=h_codes[:, grp, tokens].bitcast(FP8X4),
+                            rhs_scale=h_scales[:, grp, tokens],
+                            start=(dp == 0),
+                            stop=(dp == PASSES - 1),
+                        )
+                nc.scalar.copy(
+                    out=ha_grouped[grp][:, ep], in_=ha_bank[:].rearrange("p slot r -> p r slot")
+                )
+
+        def quantise_ha(grp):
+            nc.vector.quantize_mx(
+                out=ha_codes[:, grp, :].bitcast(FP8X4),
+                scales=ha_scales[:, grp, :],
+                in_=ha_grouped[grp][:].rearrange("p c r slot -> p (c r slot)"),
+            )
+
+        def second_matmul(r):
+            score_banks[r] = score_psum.tile([P, ROUND, P], F32, name="score_bank")
+            for i in range(ROUND):
+                grp = r * ROUND + i
+                for ep in range(PASSES):
+                    tokens = slice(ep * P, (ep + 1) * P)
+                    nc.tensor.matmul_mx(
+                        out=score_banks[r][:, i, :],
+                        lhsT=ha_codes[:, grp, tokens].bitcast(FP8X4),
+                        lhsT_scale=ha_scales[:, grp, tokens],
+                        rhs=h_codes[:, grp, tokens].bitcast(FP8X4),
+                        rhs_scale=h_scales[:, grp, tokens],
+                        start=(ep == 0),
+                        stop=(ep == PASSES - 1),
+                    )
+
+        def softmax_to_exp(r):
+            masked = soft.tile([P, ROUND, T], F32)
+            for b in range(SEQS_IN_GROUP):
+                own = slice(b * T, (b + 1) * T)
+                nc.vector.tensor_tensor(
+                    out=masked[own, :, :],
+                    in0=score_banks[r][own, :, own],
+                    in1=mask[own, own].unsqueeze(1).to_broadcast([T, ROUND, T]),
+                    op=ALU.add,
+                )
+            row_max = soft.tile([P, ROUND], F32)
+            nc.vector.tensor_reduce(out=row_max[:], in_=masked[:], axis=AXIS.X, op=ALU.max)
+            shifted = soft.tile([P, ROUND, T], F32)
+            nc.vector.tensor_tensor(
+                out=shifted[:],
+                in0=masked[:],
+                in1=row_max[:].unsqueeze(2).to_broadcast([P, ROUND, T]),
+                op=ALU.subtract,
+            )
+            exps[r] = soft.tile([P, ROUND, T], F32, name="exps")
+            nc.scalar.activation(out=exps[r][:], in_=shifted[:], func=ACT.Exp)
+
+        def softmax_from_exp(r):
+            groups = slice(r * ROUND, (r + 1) * ROUND)
+            row_sum = soft.tile([P, ROUND], F32)
+            nc.vector.tensor_reduce(out=row_sum[:], in_=exps[r][:], axis=AXIS.X, op=ALU.add)
+            inverse = soft.tile([P, ROUND], F32)
+            nc.vector.reciprocal(out=inverse[:], in_=row_sum[:])
+            nc.vector.tensor_tensor(
+                out=attn[:, groups, :],
+                in0=exps[r][:],
+                in1=inverse[:].unsqueeze(2).to_broadcast([P, ROUND, T]),
+                op=ALU.mult,
+            )
+            nc.sync.dma_start(out=out_rows[:, groups, :], in_=attn[:, groups, :])
+
+        transpose_round(0)
+        copy_h(0)
+        quantise_h(0)
+        quantise_a()
+        for grp in range(1, ROUND):
+            copy_h(grp)
+        for grp in range(1, ROUND):
+            quantise_h(grp)
+
+        for r in range(ROUNDS + 1):
+            multiply = r < ROUNDS
+            prepare = r + 1 < ROUNDS
+            finish = r > 0
+            first = r * ROUND
+
+            if multiply:
+                first_matmul(first)
+            if finish:
+                quantise_ha(first - 1)
+            if prepare:
+                transpose_round(r + 1)
+                for grp in range(first + ROUND, first + 2 * ROUND):
+                    copy_h(grp)
+            if multiply:
+                first_matmul(first + 1)
+                quantise_ha(first)
+            if finish:
+                second_matmul(r - 1)
+            if prepare:
+                for grp in range(first + ROUND, first + 2 * ROUND):
+                    quantise_h(grp)
+            if multiply:
+                first_matmul(first + 2)
+            if finish:
+                softmax_to_exp(r - 1)
+            if multiply:
+                quantise_ha(first + 1)
+                first_matmul(first + 3)
+            if finish:
+                softmax_from_exp(r - 1)
+            if multiply:
+                quantise_ha(first + 2)

@@ -38,6 +38,8 @@ def tile_causalselfattention_pa_t_kernel(tc, h, A, out):
         ha_psum = ctx.enter_context(tc.psum_pool(name="ha_psum", bufs=3))
         score_psum = ctx.enter_context(tc.psum_pool(name="score_psum", bufs=1))
 
+        ctx.enter_context(tc.manual_schedule())
+
         identity = keep.tile([P, P], F32)
         make_identity(nc, identity[:])
         mask = keep.tile([P, P], F32)

@@ -34,8 +34,7 @@ def tile_causalselfattention_pa_t_kernel(tc, h, A, out):
         h_stage = ctx.enter_context(tc.tile_pool(name="h_stage", bufs=2 * ROUND))
         ha_stage = ctx.enter_context(tc.tile_pool(name="ha_stage", bufs=ROUND))
         soft = ctx.enter_context(tc.tile_pool(name="soft", bufs=2))
-        xt_psum = ctx.enter_context(tc.psum_pool(name="xt_psum", bufs=ROUND))
-        ha_psum = ctx.enter_context(tc.psum_pool(name="ha_psum", bufs=3))
+        bank_psum = ctx.enter_context(tc.psum_pool(name="bank_psum", bufs=7))
         score_psum = ctx.enter_context(tc.psum_pool(name="score_psum", bufs=1))
 
         ctx.enter_context(tc.manual_schedule())
@@ -89,11 +88,16 @@ def tile_causalselfattention_pa_t_kernel(tc, h, A, out):
         h_grouped = {}
         ha_grouped = {}
         score_banks = {}
+        masked = {}
+        row_max = {}
+        shifted = {}
         exps = {}
+        row_sum = {}
+        inverse = {}
 
         def transpose_round(r):
             for grp in range(r * ROUND, (r + 1) * ROUND):
-                xt_banks[grp] = xt_psum.tile([P, PACK, P], F32, name="xt_bank")
+                xt_banks[grp] = bank_psum.tile([P, PACK, P], F32, name="xt_bank", tag="bank")
                 for quarter in range(PACK):
                     first_word = grp * WORDS + quarter * P
                     nc.tensor.transpose(
@@ -137,11 +141,12 @@ def tile_causalselfattention_pa_t_kernel(tc, h, A, out):
                 for u in range(2):
                     first_col = ep * K_PASS + u * 2 * P
                     src = a_raw[:, dp, :, first_col : first_col + 2 * P]
-                    src = src.rearrange("p j (q v) -> p v q j", v=2)
+                    src = src.rearrange("p j (q v) -> p q j v", v=2)
+                    dst = grouped[dp, ep][:, u].rearrange("p v q j -> p q j v")
                     if u == 0:
-                        nc.vector.tensor_copy(out=grouped[dp, ep][:, u], in_=src)
+                        nc.vector.tensor_copy(out=dst, in_=src)
                     else:
-                        nc.scalar.copy(out=grouped[dp, ep][:, u], in_=src)
+                        nc.scalar.copy(out=dst, in_=src)
                 if i > 0:
                     quantise_piece(*pieces[i - 1])
             quantise_piece(*pieces[-1])
@@ -149,7 +154,7 @@ def tile_causalselfattention_pa_t_kernel(tc, h, A, out):
         def first_matmul(grp):
             ha_grouped[grp] = ha_stage.tile([P, PASSES, P, PACK], BF16, align_bytes=64, name="ha_grouped")
             for ep in range(PASSES):
-                ha_bank = ha_psum.tile([P, PACK, P], F32)
+                ha_bank = bank_psum.tile([P, PACK, P], F32, name="ha_bank", tag="bank")
                 for slot in range(PACK):
                     places = slice((ep * PACK + slot) * P, (ep * PACK + slot + 1) * P)
                     for dp in range(PASSES):
@@ -190,38 +195,48 @@ def tile_causalselfattention_pa_t_kernel(tc, h, A, out):
                         stop=(ep == PASSES - 1),
                     )
 
-        def softmax_to_exp(r):
-            masked = soft.tile([P, ROUND, T], F32)
+        def take_out_scores(r):
+            masked[r] = soft.tile([P, ROUND, T], F32, name="masked")
             for b in range(SEQS_IN_GROUP):
                 own = slice(b * T, (b + 1) * T)
                 nc.vector.tensor_tensor(
-                    out=masked[own, :, :],
+                    out=masked[r][own, :, :],
                     in0=score_banks[r][own, :, own],
                     in1=mask[own, own].unsqueeze(1).to_broadcast([T, ROUND, T]),
                     op=ALU.add,
                 )
-            row_max = soft.tile([P, ROUND], F32)
-            nc.vector.tensor_reduce(out=row_max[:], in_=masked[:], axis=AXIS.X, op=ALU.max)
-            shifted = soft.tile([P, ROUND, T], F32)
+
+        def row_maxima(r):
+            row_max[r] = soft.tile([P, ROUND], F32, name="row_max")
+            nc.vector.tensor_reduce(out=row_max[r][:], in_=masked[r][:], axis=AXIS.X, op=ALU.max)
+
+        def subtract_maxima(r):
+            shifted[r] = soft.tile([P, ROUND, T], F32, name="shifted")
             nc.vector.tensor_tensor(
-                out=shifted[:],
-                in0=masked[:],
-                in1=row_max[:].unsqueeze(2).to_broadcast([P, ROUND, T]),
+                out=shifted[r][:],
+                in0=masked[r][:],
+                in1=row_max[r][:].unsqueeze(2).to_broadcast([P, ROUND, T]),
                 op=ALU.subtract,
             )
-            exps[r] = soft.tile([P, ROUND, T], F32, name="exps")
-            nc.scalar.activation(out=exps[r][:], in_=shifted[:], func=ACT.Exp)
 
-        def softmax_from_exp(r):
+        def exponentials(r):
+            exps[r] = soft.tile([P, ROUND, T], F32, name="exps")
+            nc.scalar.activation(out=exps[r][:], in_=shifted[r][:], func=ACT.Exp)
+
+        def row_sums(r):
+            row_sum[r] = soft.tile([P, ROUND], F32, name="row_sum")
+            nc.vector.tensor_reduce(out=row_sum[r][:], in_=exps[r][:], axis=AXIS.X, op=ALU.add)
+
+        def invert_sums(r):
+            inverse[r] = soft.tile([P, ROUND], F32, name="inverse")
+            nc.vector.reciprocal(out=inverse[r][:], in_=row_sum[r][:])
+
+        def normalise_and_store(r):
             groups = slice(r * ROUND, (r + 1) * ROUND)
-            row_sum = soft.tile([P, ROUND], F32)
-            nc.vector.tensor_reduce(out=row_sum[:], in_=exps[r][:], axis=AXIS.X, op=ALU.add)
-            inverse = soft.tile([P, ROUND], F32)
-            nc.vector.reciprocal(out=inverse[:], in_=row_sum[:])
             nc.vector.tensor_tensor(
                 out=attn[:, groups, :],
                 in0=exps[r][:],
-                in1=inverse[:].unsqueeze(2).to_broadcast([P, ROUND, T]),
+                in1=inverse[r][:].unsqueeze(2).to_broadcast([P, ROUND, T]),
                 op=ALU.mult,
             )
             nc.sync.dma_start(out=out_rows[:, groups, :], in_=attn[:, groups, :])
@@ -235,36 +250,52 @@ def tile_causalselfattention_pa_t_kernel(tc, h, A, out):
         for grp in range(1, ROUND):
             quantise_h(grp)
 
-        for r in range(ROUNDS + 1):
+        for r in range(ROUNDS + 2):
             multiply = r < ROUNDS
             prepare = r + 1 < ROUNDS
-            finish = r > 0
+            score = 1 <= r <= ROUNDS
+            finish = r >= 2
             first = r * ROUND
+            coming = first + ROUND
 
             if multiply:
                 first_matmul(first)
-            if finish:
+            if score:
                 quantise_ha(first - 1)
+            if finish:
+                exponentials(r - 2)
             if prepare:
                 transpose_round(r + 1)
-                for grp in range(first + ROUND, first + 2 * ROUND):
-                    copy_h(grp)
+                copy_h(coming)
+                copy_h(coming + 1)
+            if finish:
+                row_sums(r - 2)
+            if prepare:
+                copy_h(coming + 2)
+            if finish:
+                invert_sums(r - 2)
+            if prepare:
+                copy_h(coming + 3)
+            if finish:
+                normalise_and_store(r - 2)
             if multiply:
                 first_matmul(first + 1)
                 quantise_ha(first)
-            if finish:
+            if score:
                 second_matmul(r - 1)
             if prepare:
-                for grp in range(first + ROUND, first + 2 * ROUND):
+                for grp in range(coming, coming + ROUND):
                     quantise_h(grp)
             if multiply:
                 first_matmul(first + 2)
-            if finish:
-                softmax_to_exp(r - 1)
+            if score:
+                take_out_scores(r - 1)
             if multiply:
                 quantise_ha(first + 1)
-                first_matmul(first + 3)
-            if finish:
-                softmax_from_exp(r - 1)
+            if score:
+                row_maxima(r - 1)
             if multiply:
+                first_matmul(first + 3)
                 quantise_ha(first + 2)
+            if score:
+                subtract_maxima(r - 1)

@@ -266,18 +266,8 @@ def tile_causalselfattention_pa_t_kernel(tc, h, A, out):
                 exponentials(r - 2)
             if prepare:
                 transpose_round(r + 1)
-                copy_h(coming)
-                copy_h(coming + 1)
-            if finish:
-                row_sums(r - 2)
-            if prepare:
-                copy_h(coming + 2)
-            if finish:
-                invert_sums(r - 2)
-            if prepare:
-                copy_h(coming + 3)
-            if finish:
-                normalise_and_store(r - 2)
+                for grp in range(coming, coming + ROUND):
+                    copy_h(grp)
             if multiply:
                 first_matmul(first + 1)
                 quantise_ha(first)
@@ -290,12 +280,18 @@ def tile_causalselfattention_pa_t_kernel(tc, h, A, out):
                 first_matmul(first + 2)
             if score:
                 take_out_scores(r - 1)
+            if finish:
+                row_sums(r - 2)
+            if score:
+                row_maxima(r - 1)
+            if finish:
+                invert_sums(r - 2)
             if multiply:
                 quantise_ha(first + 1)
             if score:
-                row_maxima(r - 1)
+                subtract_maxima(r - 1)
+            if finish:
+                normalise_and_store(r - 2)
             if multiply:
                 first_matmul(first + 3)
                 quantise_ha(first + 2)
-            if score:
-                subtract_maxima(r - 1)

@@ -61,7 +61,7 @@ def tile_causalselfattention_pa_t_kernel(tc, h, A, out):
         h_words = h_raw[:].rearrange("p g d -> p (g d)").bitcast(F32)
         h_codes = keep.tile([P, GROUPS, PASSES * P], U32, align_bytes=64)
         h_scales = keep.tile([P, GROUPS, PASSES * P], U8, align_bytes=64)
-        a_raw = keep.tile([P, PASSES, PACK, D], BF16)
+        a_raw = keep.tile([P, PASSES, PASSES, PACK, K_PASS], BF16)
         a_codes = keep.tile([P, PASSES, D], U32, align_bytes=64)
         a_scales = keep.tile([P, PASSES, D], U8, align_bytes=64)
         ha_codes = keep.tile([P, GROUPS, PASSES * P], U32, align_bytes=64)
@@ -69,24 +69,35 @@ def tile_causalselfattention_pa_t_kernel(tc, h, A, out):
         attn = keep.tile([P, GROUPS, T], F32)
 
         h_rows = h.rearrange("b t d -> (b t) d").rearrange("(g p) d -> p g d", p=P)
-        a_rows = A.rearrange("n (c u p v) e -> p (n c) u (v e)", c=PASSES, u=2, v=2)
+        a_rows = A.rearrange("n (c u p v) e -> p (n c) u v e", c=PASSES, u=2, v=2)
         out_rows = out.rearrange("(g b) n t s -> (b n t) g s", b=SEQS_IN_GROUP)
 
         def load_h(first, last):
             nc.sync.dma_start(out=h_raw[:, first:last, :], in_=h_rows[:, first:last, :])
 
+        def load_a(ep):
+            for dp in range(PASSES):
+                for u in range(2):
+                    nc.sync.dma_start(
+                        out=a_raw[:, ep, dp, 2 * u : 2 * u + 2, :],
+                        in_=a_rows[:, dp, u, :, ep * K_PASS : (ep + 1) * K_PASS],
+                    )
+
         load_h(0, 1)
-        for dp in range(PASSES):
-            nc.sync.dma_start(
-                out=a_raw[:, dp].rearrange("p (u v) e -> p u (v e)", u=2), in_=a_rows[:, dp]
-            )
-        load_h(1, ROUND)
-        for r in range(1, ROUNDS):
+        load_a(0)
+        for grp in range(1, ROUND):
+            load_h(grp, grp + 1)
+        load_a(1)
+        for grp in range(ROUND, 2 * ROUND):
+            load_h(grp, grp + 1)
+        for r in range(2, ROUNDS):
             load_h(r * ROUND, (r + 1) * ROUND)
 
         xt_banks = {}
         h_grouped = {}
         ha_grouped = {}
+        ha_banks = {}
+        a_grouped = {}
         score_banks = {}
         masked = {}
         row_max = {}
@@ -95,22 +106,21 @@ def tile_causalselfattention_pa_t_kernel(tc, h, A, out):
         row_sum = {}
         inverse = {}
 
-        def transpose_round(r):
-            for grp in range(r * ROUND, (r + 1) * ROUND):
-                xt_banks[grp] = bank_psum.tile([P, PACK, P], F32, name="xt_bank", tag="bank")
-                for quarter in range(PACK):
-                    first_word = grp * WORDS + quarter * P
-                    nc.tensor.transpose(
-                        xt_banks[grp][:, quarter, :],
-                        h_words[:, first_word : first_word + P],
-                        identity[:],
-                    )
+        def transpose_group(grp):
+            xt_banks[grp] = bank_psum.tile([P, PACK, P], F32, name="xt_bank", tag="bank")
+            for quarter in range(PACK):
+                first_word = grp * WORDS + quarter * P
+                nc.tensor.transpose(
+                    xt_banks[grp][:, quarter, :],
+                    h_words[:, first_word : first_word + P],
+                    identity[:],
+                )
 
-        def copy_h(grp):
+        def copy_h(grp, on_scalar):
             h_grouped[grp] = h_stage.tile([P, PASSES * P * PACK], BF16, align_bytes=64, name="h_grouped")
             pairs_out = h_grouped[grp][:].bitcast(F32).rearrange("p (c r u) -> p c r u", c=PASSES, u=2)
             pairs_in = xt_banks[grp][:].rearrange("p (c u) r -> p c r u", u=2)
-            if grp % ROUND == 0:
+            if on_scalar:
                 nc.scalar.copy(out=pairs_out, in_=pairs_in)
             else:
                 nc.vector.tensor_copy(out=pairs_out, in_=pairs_in)
@@ -122,55 +132,56 @@ def tile_causalselfattention_pa_t_kernel(tc, h, A, out):
                 in_=h_grouped[grp][:],
             )
 
-        def quantise_a():
-            pieces = [(dp, ep) for dp in range(PASSES) for ep in range(PASSES)]
-            grouped = {}
+        def copy_a(dp, ep):
+            a_grouped[dp, ep] = keep.tile(
+                [P, 2, 2, P, PACK], BF16, align_bytes=64, name="a_grouped%d%d" % (dp, ep)
+            )
+            for u in range(2):
+                src = a_raw[:, ep, dp, :, u * 2 * P : (u + 1) * 2 * P]
+                src = src.rearrange("p j (q v) -> p q j v", v=2)
+                dst = a_grouped[dp, ep][:, u].rearrange("p v q j -> p q j v")
+                if u == 0:
+                    nc.vector.tensor_copy(out=dst, in_=src)
+                else:
+                    nc.scalar.copy(out=dst, in_=src)
 
-            def quantise_piece(dp, ep):
-                places = slice(ep * K_PASS, (ep + 1) * K_PASS)
-                nc.vector.quantize_mx(
-                    out=a_codes[:, dp, places].bitcast(FP8X4),
-                    scales=a_scales[:, dp, places],
-                    in_=grouped[dp, ep][:].rearrange("p u v q j -> p (u v q j)"),
-                )
+        def quantise_a(dp, ep):
+            places = slice(ep * K_PASS, (ep + 1) * K_PASS)
+            nc.vector.quantize_mx(
+                out=a_codes[:, dp, places].bitcast(FP8X4),
+                scales=a_scales[:, dp, places],
+                in_=a_grouped[dp, ep][:].rearrange("p u v q j -> p (u v q j)"),
+            )
 
-            for i, (dp, ep) in enumerate(pieces):
-                grouped[dp, ep] = keep.tile(
-                    [P, 2, 2, P, PACK], BF16, align_bytes=64, name="a_grouped%d%d" % (dp, ep)
-                )
-                for u in range(2):
-                    first_col = ep * K_PASS + u * 2 * P
-                    src = a_raw[:, dp, :, first_col : first_col + 2 * P]
-                    src = src.rearrange("p j (q v) -> p q j v", v=2)
-                    dst = grouped[dp, ep][:, u].rearrange("p v q j -> p q j v")
-                    if u == 0:
-                        nc.vector.tensor_copy(out=dst, in_=src)
-                    else:
-                        nc.scalar.copy(out=dst, in_=src)
-                if i > 0:
-                    quantise_piece(*pieces[i - 1])
-            quantise_piece(*pieces[-1])
+        def multiply(grp, ep):
+            ha_banks[grp, ep] = bank_psum.tile([P, PACK, P], F32, name="ha_bank", tag="bank")
+            for slot in range(PACK):
+                places = slice((ep * PACK + slot) * P, (ep * PACK + slot + 1) * P)
+                for dp in range(PASSES):
+                    tokens = slice(dp * P, (dp + 1) * P)
+                    nc.tensor.matmul_mx(
+                        out=ha_banks[grp, ep][:, slot, :],
+                        lhsT=a_codes[:, dp, places].bitcast(FP8X4),
+                        lhsT_scale=a_scales[:, dp, places],
+                        rhs=h_codes[:, grp, tokens].bitcast(FP8X4),
+                        rhs_scale=h_scales[:, grp, tokens],
+                        start=(dp == 0),
+                        stop=(dp == PASSES - 1),
+                    )
+
+        def copy_ha(grp, ep, on_vector=False):
+            if ep == 0:
+                ha_grouped[grp] = ha_stage.tile([P, PASSES, P, PACK], BF16, align_bytes=64, name="ha_grouped")
+            words_in = ha_banks[grp, ep][:].rearrange("p slot r -> p r slot")
+            if on_vector:
+                nc.vector.tensor_copy(out=ha_grouped[grp][:, ep], in_=words_in)
+            else:
+                nc.scalar.copy(out=ha_grouped[grp][:, ep], in_=words_in)
 
         def first_matmul(grp):
-            ha_grouped[grp] = ha_stage.tile([P, PASSES, P, PACK], BF16, align_bytes=64, name="ha_grouped")
             for ep in range(PASSES):
-                ha_bank = bank_psum.tile([P, PACK, P], F32, name="ha_bank", tag="bank")
-                for slot in range(PACK):
-                    places = slice((ep * PACK + slot) * P, (ep * PACK + slot + 1) * P)
-                    for dp in range(PASSES):
-                        tokens = slice(dp * P, (dp + 1) * P)
-                        nc.tensor.matmul_mx(
-                            out=ha_bank[:, slot, :],
-                            lhsT=a_codes[:, dp, places].bitcast(FP8X4),
-                            lhsT_scale=a_scales[:, dp, places],
-                            rhs=h_codes[:, grp, tokens].bitcast(FP8X4),
-                            rhs_scale=h_scales[:, grp, tokens],
-                            start=(dp == 0),
-                            stop=(dp == PASSES - 1),
-                        )
-                nc.scalar.copy(
-                    out=ha_grouped[grp][:, ep], in_=ha_bank[:].rearrange("p slot r -> p r slot")
-                )
+                multiply(grp, ep)
+                copy_ha(grp, ep)
 
         def quantise_ha(grp):
             nc.vector.quantize_mx(
@@ -241,34 +252,71 @@ def tile_causalselfattention_pa_t_kernel(tc, h, A, out):
             )
             nc.sync.dma_start(out=out_rows[:, groups, :], in_=attn[:, groups, :])
 
-        transpose_round(0)
-        copy_h(0)
+        transpose_group(0)
+        copy_h(0, False)
+        copy_a(0, 0)
         quantise_h(0)
-        quantise_a()
+        copy_a(1, 0)
+        quantise_a(0, 0)
         for grp in range(1, ROUND):
-            copy_h(grp)
-        for grp in range(1, ROUND):
+            transpose_group(grp)
+        copy_h(1, False)
+        quantise_a(1, 0)
+        multiply(0, 0)
+        copy_h(2, True)
+        copy_h(3, False)
+        quantise_h(1)
+        multiply(1, 0)
+        quantise_h(2)
+        multiply(2, 0)
+        quantise_h(3)
+        multiply(3, 0)
+        copy_a(0, 1)
+        copy_ha(0, 0)
+        copy_a(1, 1)
+        quantise_a(0, 1)
+        copy_ha(1, 0)
+        copy_ha(2, 0, True)
+        quantise_a(1, 1)
+        copy_ha(3, 0)
+        for grp in range(ROUND, 2 * ROUND):
+            transpose_group(grp)
+        for grp in range(ROUND, 2 * ROUND):
+            copy_h(grp, grp == ROUND)
+        multiply(0, 1)
+        copy_ha(0, 1)
+        multiply(1, 1)
+        copy_ha(1, 1)
+        quantise_ha(0)
+        for grp in range(ROUND, 2 * ROUND):
             quantise_h(grp)
+        multiply(2, 1)
+        copy_ha(2, 1)
+        quantise_ha(1)
+        multiply(3, 1)
+        copy_ha(3, 1)
+        quantise_ha(2)
 
-        for r in range(ROUNDS + 2):
-            multiply = r < ROUNDS
+        for r in range(1, ROUNDS + 2):
+            multiply_turn = r < ROUNDS
             prepare = r + 1 < ROUNDS
             score = 1 <= r <= ROUNDS
             finish = r >= 2
             first = r * ROUND
             coming = first + ROUND
 
-            if multiply:
+            if multiply_turn:
                 first_matmul(first)
             if score:
                 quantise_ha(first - 1)
             if finish:
                 exponentials(r - 2)
             if prepare:
-                transpose_round(r + 1)
                 for grp in range(coming, coming + ROUND):
-                    copy_h(grp)
-            if multiply:
+                    transpose_group(grp)
+                for grp in range(coming, coming + ROUND):
+                    copy_h(grp, grp == coming)
+            if multiply_turn:
                 first_matmul(first + 1)
                 quantise_ha(first)
             if score:
@@ -276,7 +324,7 @@ def tile_causalselfattention_pa_t_kernel(tc, h, A, out):
             if prepare:
                 for grp in range(coming, coming + ROUND):
                     quantise_h(grp)
-            if multiply:
+            if multiply_turn:
                 first_matmul(first + 2)
             if score:
                 take_out_scores(r - 1)
@@ -286,12 +334,12 @@ def tile_causalselfattention_pa_t_kernel(tc, h, A, out):
                 row_maxima(r - 1)
             if finish:
                 invert_sums(r - 2)
-            if multiply:
+            if multiply_turn:
                 quantise_ha(first + 1)
             if score:
                 subtract_maxima(r - 1)
             if finish:
                 normalise_and_store(r - 2)
-            if multiply:
+            if multiply_turn:
                 first_matmul(first + 3)
                 quantise_ha(first + 2)

@@ -48,7 +48,7 @@ def tile_causalselfattention_pa_t_kernel(tc, h, A, out):
             in_=mask[:],
             pattern=[[-1, P]],
             compare_op=ALU.is_ge,
-            fill=NEG_INF,
+            fill=-NEG_INF,
             base=0,
             channel_multiplier=1,
         )
@@ -99,9 +99,8 @@ def tile_causalselfattention_pa_t_kernel(tc, h, A, out):
         ha_banks = {}
         a_grouped = {}
         score_banks = {}
-        masked = {}
-        row_max = {}
-        shifted = {}
+        negated = {}
+        row_min = {}
         exps = {}
         row_sum = {}
         inverse = {}
@@ -207,36 +206,32 @@ def tile_causalselfattention_pa_t_kernel(tc, h, A, out):
                     )
 
         def take_out_scores(r):
-            masked[r] = soft.tile([P, ROUND, T], F32, name="masked")
+            negated[r] = soft.tile([P, ROUND, T], F32, name="negated")
             for b in range(SEQS_IN_GROUP):
                 own = slice(b * T, (b + 1) * T)
                 nc.vector.tensor_tensor(
-                    out=masked[r][own, :, :],
-                    in0=score_banks[r][own, :, own],
-                    in1=mask[own, own].unsqueeze(1).to_broadcast([T, ROUND, T]),
-                    op=ALU.add,
+                    out=negated[r][own, :, :],
+                    in0=mask[own, own].unsqueeze(1).to_broadcast([T, ROUND, T]),
+                    in1=score_banks[r][own, :, own],
+                    op=ALU.subtract,
                 )
 
-        def row_maxima(r):
-            row_max[r] = soft.tile([P, ROUND], F32, name="row_max")
-            nc.vector.tensor_reduce(out=row_max[r][:], in_=masked[r][:], axis=AXIS.X, op=ALU.max)
-
-        def subtract_maxima(r):
-            shifted[r] = soft.tile([P, ROUND, T], F32, name="shifted")
-            nc.vector.tensor_tensor(
-                out=shifted[r][:],
-                in0=masked[r][:],
-                in1=row_max[r][:].unsqueeze(2).to_broadcast([P, ROUND, T]),
-                op=ALU.subtract,
-            )
+        def row_minima(r):
+            row_min[r] = soft.tile([P, ROUND], F32, name="row_min")
+            nc.vector.tensor_reduce(out=row_min[r][:], in_=negated[r][:], axis=AXIS.X, op=ALU.min)
 
         def exponentials(r):
             exps[r] = soft.tile([P, ROUND, T], F32, name="exps")
-            nc.scalar.activation(out=exps[r][:], in_=shifted[r][:], func=ACT.Exp)
-
-        def row_sums(r):
             row_sum[r] = soft.tile([P, ROUND], F32, name="row_sum")
-            nc.vector.tensor_reduce(out=row_sum[r][:], in_=exps[r][:], axis=AXIS.X, op=ALU.add)
+            for i in range(ROUND):
+                nc.scalar.activation(
+                    out=exps[r][:, i, :],
+                    in_=negated[r][:, i, :],
+                    func=ACT.Exp,
+                    scale=-1.0,
+                    bias=row_min[r][:, i : i + 1],
+                    accum_out=row_sum[r][:, i : i + 1],
+                )
 
         def invert_sums(r):
             inverse[r] = soft.tile([P, ROUND], F32, name="inverse")
@@ -329,15 +324,11 @@ def tile_causalselfattention_pa_t_kernel(tc, h, A, out):
             if score:
                 take_out_scores(r - 1)
             if finish:
-                row_sums(r - 2)
-            if score:
-                row_maxima(r - 1)
-            if finish:
                 invert_sums(r - 2)
             if multiply_turn:
                 quantise_ha(first + 1)
             if score:
-                subtract_maxima(r - 1)
+                row_minima(r - 1)
             if finish:
                 normalise_and_store(r - 2)
             if multiply_turn:

@@ -57,6 +57,9 @@ def tile_causalselfattention_pa_t_kernel(tc, h, A, out):
         nc.vector.memset(table_in[:], 0.0)
         nc.scalar.activation(out=table_out[:], in_=table_in[:], func=ACT.Exp)
 
+        idle_in = keep.tile([P, K_PASS], BF16)
+        nc.vector.memset(idle_in[:], 0.0)
+
         h_raw = keep.tile([P, GROUPS, D], BF16)
         h_words = h_raw[:].rearrange("p g d -> p (g d)").bitcast(F32)
         h_codes = keep.tile([P, GROUPS, PASSES * P], U32, align_bytes=64)
@@ -114,6 +117,10 @@ def tile_causalselfattention_pa_t_kernel(tc, h, A, out):
                     h_words[:, first_word : first_word + P],
                     identity[:],
                 )
+
+        def idle_matmuls(count):
+            for i in range(count):
+                nc.tensor.matmul(idle_bank[0][:], lhsT=idle_in[:, 0:P], rhs=idle_in[:], start=True, stop=True)
 
         def copy_h(grp, on_scalar):
             h_grouped[grp] = h_stage.tile([P, PASSES * P * PACK], BF16, align_bytes=64, name="h_grouped")
@@ -248,6 +255,8 @@ def tile_causalselfattention_pa_t_kernel(tc, h, A, out):
             nc.sync.dma_start(out=out_rows[:, groups, :], in_=attn[:, groups, :])
 
         transpose_group(0)
+        idle_bank = [bank_psum.tile([P, K_PASS], F32, name="idle_bank", tag="bank")]
+        idle_matmuls(5)
         copy_h(0, False)
         copy_a(0, 0)
         quantise_h(0)
@@ -255,6 +264,8 @@ def tile_causalselfattention_pa_t_kernel(tc, h, A, out):
         quantise_a(0, 0)
         for grp in range(1, ROUND):
             transpose_group(grp)
+            if grp + 1 < ROUND:
+                idle_matmuls(1)
         copy_h(1, False)
         quantise_a(1, 0)
         multiply(0, 0)

@@ -318,9 +318,9 @@ def tile_causalselfattention_pa_t_kernel(tc, h, A, out):
             if finish:
                 exponentials(r - 2)
             if prepare:
-                for grp in range(coming, coming + ROUND):
+                for grp in range(coming, coming + 2):
                     transpose_group(grp)
-                for grp in range(coming, coming + ROUND):
+                for grp in range(coming, coming + 2):
                     copy_h(grp, grp == coming)
             if multiply_turn:
                 first_matmul(first + 1)
@@ -328,7 +328,7 @@ def tile_causalselfattention_pa_t_kernel(tc, h, A, out):
             if score:
                 second_matmul(r - 1)
             if prepare:
-                for grp in range(coming, coming + ROUND):
+                for grp in range(coming, coming + 2):
                     quantise_h(grp)
             if multiply_turn:
                 first_matmul(first + 2)
@@ -336,6 +336,11 @@ def tile_causalselfattention_pa_t_kernel(tc, h, A, out):
                 take_out_scores(r - 1)
             if finish:
                 invert_sums(r - 2)
+            if prepare:
+                for grp in range(coming + 2, coming + ROUND):
+                    transpose_group(grp)
+                for grp in range(coming + 2, coming + ROUND):
+                    copy_h(grp, False)
             if multiply_turn:
                 quantise_ha(first + 1)
             if score:
@@ -344,4 +349,8 @@ def tile_causalselfattention_pa_t_kernel(tc, h, A, out):
                 normalise_and_store(r - 2)
             if multiply_turn:
                 first_matmul(first + 3)
+            if prepare:
+                for grp in range(coming + 2, coming + ROUND):
+                    quantise_h(grp)
+            if multiply_turn:
                 quantise_ha(first + 2)

@@ -31,8 +31,8 @@ def tile_causalselfattention_pa_t_kernel(tc, h, A, out):
     nc = tc.nc
     with ExitStack() as ctx:
         keep = ctx.enter_context(tc.tile_pool(name="keep", bufs=1))
-        h_stage = ctx.enter_context(tc.tile_pool(name="h_stage", bufs=2 * ROUND))
-        ha_stage = ctx.enter_context(tc.tile_pool(name="ha_stage", bufs=ROUND))
+        h_stage = ctx.enter_context(tc.tile_pool(name="h_stage", bufs=ROUND))
+        ha_stage = ctx.enter_context(tc.tile_pool(name="ha_stage", bufs=3))
         soft = ctx.enter_context(tc.tile_pool(name="soft", bufs=2))
         bank_psum = ctx.enter_context(tc.psum_pool(name="bank_psum", bufs=7))
         score_psum = ctx.enter_context(tc.psum_pool(name="score_psum", bufs=1))
@@ -123,19 +123,22 @@ def tile_causalselfattention_pa_t_kernel(tc, h, A, out):
                 nc.tensor.matmul(idle_bank[0][:], lhsT=idle_in[:, 0:P], rhs=idle_in[:], start=True, stop=True)
 
         def copy_h(grp, on_scalar):
-            h_grouped[grp] = h_stage.tile([P, PASSES * P * PACK], BF16, align_bytes=64, name="h_grouped")
-            pairs_out = h_grouped[grp][:].bitcast(F32).rearrange("p (c r u) -> p c r u", c=PASSES, u=2)
+            if grp % 2 == 0:
+                h_grouped[grp // 2] = h_stage.tile([P, 2, PASSES * P * PACK], BF16, align_bytes=64, name="h_grouped")
+            pairs_out = h_grouped[grp // 2][:, grp % 2].bitcast(F32).rearrange("p (c r u) -> p c r u", c=PASSES, u=2)
             pairs_in = xt_banks[grp][:].rearrange("p (c u) r -> p c r u", u=2)
             if on_scalar:
                 nc.scalar.copy(out=pairs_out, in_=pairs_in)
             else:
                 nc.vector.tensor_copy(out=pairs_out, in_=pairs_in)
 
-        def quantise_h(grp):
+        def quantise_h(grp, count=1):
+            groups = slice(grp, grp + count)
+            halves = slice(grp % 2, grp % 2 + count)
             nc.vector.quantize_mx(
-                out=h_codes[:, grp, :].bitcast(FP8X4),
-                scales=h_scales[:, grp, :],
-                in_=h_grouped[grp][:],
+                out=h_codes[:, groups, :].rearrange("p g w -> p (g w)").bitcast(FP8X4),
+                scales=h_scales[:, groups, :].rearrange("p g w -> p (g w)"),
+                in_=h_grouped[grp // 2][:, halves].rearrange("p g k -> p (g k)"),
             )
 
         def copy_a(dp, ep):
@@ -176,24 +179,26 @@ def tile_causalselfattention_pa_t_kernel(tc, h, A, out):
                     )
 
         def copy_ha(grp, ep, on_vector=False):
-            if ep == 0:
-                ha_grouped[grp] = ha_stage.tile([P, PASSES, P, PACK], BF16, align_bytes=64, name="ha_grouped")
+            if ep == 0 and grp % 2 == 0:
+                ha_grouped[grp // 2] = ha_stage.tile([P, 2, PASSES, P, PACK], BF16, align_bytes=64, name="ha_grouped")
             words_in = ha_banks[grp, ep][:].rearrange("p slot r -> p r slot")
             if on_vector:
-                nc.vector.tensor_copy(out=ha_grouped[grp][:, ep], in_=words_in)
+                nc.vector.tensor_copy(out=ha_grouped[grp // 2][:, grp % 2, ep], in_=words_in)
             else:
-                nc.scalar.copy(out=ha_grouped[grp][:, ep], in_=words_in)
+                nc.scalar.copy(out=ha_grouped[grp // 2][:, grp % 2, ep], in_=words_in)
 
         def first_matmul(grp):
             for ep in range(PASSES):
                 multiply(grp, ep)
                 copy_ha(grp, ep)
 
-        def quantise_ha(grp):
+        def quantise_ha(grp, count=1):
+            groups = slice(grp, grp + count)
+            halves = slice(grp % 2, grp % 2 + count)
             nc.vector.quantize_mx(
-                out=ha_codes[:, grp, :].bitcast(FP8X4),
-                scales=ha_scales[:, grp, :],
-                in_=ha_grouped[grp][:].rearrange("p c r slot -> p (c r slot)"),
+                out=ha_codes[:, groups, :].rearrange("p g w -> p (g w)").bitcast(FP8X4),
+                scales=ha_scales[:, groups, :].rearrange("p g w -> p (g w)"),
+                in_=ha_grouped[grp // 2][:, halves].rearrange("p g c r slot -> p (g c r slot)"),
             )
 
         def second_matmul(r):
@@ -293,15 +298,13 @@ def tile_causalselfattention_pa_t_kernel(tc, h, A, out):
         copy_ha(0, 1)
         multiply(1, 1)
         copy_ha(1, 1)
-        quantise_ha(0)
-        for grp in range(ROUND, 2 * ROUND):
-            quantise_h(grp)
+        for grp in range(ROUND, 2 * ROUND, 2):
+            quantise_h(grp, 2)
         multiply(2, 1)
         copy_ha(2, 1)
-        quantise_ha(1)
+        quantise_ha(0, 2)
         multiply(3, 1)
         copy_ha(3, 1)
-        quantise_ha(2)
 
         for r in range(1, ROUNDS + 2):
             multiply_turn = r < ROUNDS
@@ -313,7 +316,9 @@ def tile_causalselfattention_pa_t_kernel(tc, h, A, out):
 
             if multiply_turn:
                 first_matmul(first)
-            if score:
+            if score and multiply_turn:
+                quantise_ha(first - 2, 2)
+            if score and not multiply_turn:
                 quantise_ha(first - 1)
             if finish:
                 exponentials(r - 2)
@@ -324,12 +329,10 @@ def tile_causalselfattention_pa_t_kernel(tc, h, A, out):
                     copy_h(grp, grp == coming)
             if multiply_turn:
                 first_matmul(first + 1)
-                quantise_ha(first)
             if score:
                 second_matmul(r - 1)
             if prepare:
-                for grp in range(coming, coming + 2):
-                    quantise_h(grp)
+                quantise_h(coming, 2)
             if multiply_turn:
                 first_matmul(first + 2)
             if score:
@@ -340,9 +343,9 @@ def tile_causalselfattention_pa_t_kernel(tc, h, A, out):
                 for grp in range(coming + 2, coming + ROUND):
                     transpose_group(grp)
                 for grp in range(coming + 2, coming + ROUND):
-                    copy_h(grp, False)
+                    copy_h(grp, grp == coming + 2)
             if multiply_turn:
-                quantise_ha(first + 1)
+                quantise_ha(first, 2)
             if score:
                 row_minima(r - 1)
             if finish:
@@ -350,7 +353,6 @@ def tile_causalselfattention_pa_t_kernel(tc, h, A, out):
             if multiply_turn:
                 first_matmul(first + 3)
             if prepare:
-                for grp in range(coming + 2, coming + ROUND):
-                    quantise_h(grp)
-            if multiply_turn:
+                quantise_h(coming + 2, 2)
+            if multiply_turn and not prepare:
                 quantise_ha(first + 2)

@@ -259,10 +259,18 @@ def tile_causalselfattention_pa_t_kernel(tc, h, A, out):
             )
             nc.sync.dma_start(out=out_rows[:, groups, :], in_=attn[:, groups, :])
 
+        def quantise_ha_half(grp, ep):
+            tokens = slice(ep * P, (ep + 1) * P)
+            nc.vector.quantize_mx(
+                out=ha_codes[:, grp, tokens].bitcast(FP8X4),
+                scales=ha_scales[:, grp, tokens],
+                in_=ha_grouped[grp // 2][:, grp % 2, ep].rearrange("p r slot -> p (r slot)"),
+            )
+
         transpose_group(0)
         idle_bank = [bank_psum.tile([P, K_PASS], F32, name="idle_bank", tag="bank")]
         idle_matmuls(5)
-        copy_h(0, False)
+        copy_h(0, True)
         copy_a(0, 0)
         quantise_h(0)
         copy_a(1, 0)
@@ -271,12 +279,12 @@ def tile_causalselfattention_pa_t_kernel(tc, h, A, out):
             transpose_group(grp)
             if grp + 1 < ROUND:
                 idle_matmuls(1)
-        copy_h(1, False)
+        copy_h(1, True)
         quantise_a(1, 0)
         multiply(0, 0)
         copy_h(2, True)
-        copy_h(3, False)
         quantise_h(1)
+        copy_h(3, False)
         multiply(1, 0)
         quantise_h(2)
         multiply(2, 0)
@@ -319,7 +327,7 @@ def tile_causalselfattention_pa_t_kernel(tc, h, A, out):
             if score and multiply_turn:
                 quantise_ha(first - 2, 2)
             if score and not multiply_turn:
-                quantise_ha(first - 1)
+                quantise_ha_half(first - 1, 1)
             if finish:
                 exponentials(r - 2)
             if prepare:
@@ -356,3 +364,4 @@ def tile_causalselfattention_pa_t_kernel(tc, h, A, out):
                 quantise_h(coming + 2, 2)
             if multiply_turn and not prepare:
                 quantise_ha(first + 2)
+                quantise_ha_half(first + 3, 0)

@@ -57,9 +57,6 @@ def tile_causalselfattention_pa_t_kernel(tc, h, A, out):
         nc.vector.memset(table_in[:], 0.0)
         nc.scalar.activation(out=table_out[:], in_=table_in[:], func=ACT.Exp)
 
-        idle_in = keep.tile([P, K_PASS], BF16)
-        nc.vector.memset(idle_in[:], 0.0)
-
         h_raw = keep.tile([P, GROUPS, D], BF16)
         h_words = h_raw[:].rearrange("p g d -> p (g d)").bitcast(F32)
         h_codes = keep.tile([P, GROUPS, PASSES * P], U32, align_bytes=64)
@@ -117,10 +114,6 @@ def tile_causalselfattention_pa_t_kernel(tc, h, A, out):
                     h_words[:, first_word : first_word + P],
                     identity[:],
                 )
-
-        def idle_matmuls(count):
-            for i in range(count):
-                nc.tensor.matmul(idle_bank[0][:], lhsT=idle_in[:, 0:P], rhs=idle_in[:], start=True, stop=True)
 
         def copy_h(grp, on_scalar):
             if grp % 2 == 0:
@@ -268,8 +261,6 @@ def tile_causalselfattention_pa_t_kernel(tc, h, A, out):
             )
 
         transpose_group(0)
-        idle_bank = [bank_psum.tile([P, K_PASS], F32, name="idle_bank", tag="bank")]
-        idle_matmuls(5)
         copy_h(0, True)
         copy_a(0, 0)
         quantise_h(0)
@@ -277,8 +268,6 @@ def tile_causalselfattention_pa_t_kernel(tc, h, A, out):
         quantise_a(0, 0)
         for grp in range(1, ROUND):
             transpose_group(grp)
-            if grp + 1 < ROUND:
-                idle_matmuls(1)
         copy_h(1, True)
         quantise_a(1, 0)
         multiply(0, 0)

from contextlib import ExitStack

import concourse.mybir as mybir
from concourse.masks import make_identity

F32 = mybir.dt.float32
BF16 = mybir.dt.bfloat16
U32 = mybir.dt.uint32
U8 = mybir.dt.uint8
FP8X4 = mybir.dt.float8_e4m3fn_x4
ALU = mybir.AluOpType
ACT = mybir.ActivationFunctionType
AXIS = mybir.AxisListType

P = 128
SEQS, T, D = 128, 32, 1024
PACK = 4
K_PASS = P * PACK
PASSES = D // K_PASS
GROUPS = SEQS * T // P
SEQS_IN_GROUP = P // T
ROUND = 4
ROUNDS = GROUPS // ROUND
WORDS = D // 2
NEG_INF = -1e30

FLOPS = 2 * SEQS * (T - 1) * D * D + 2 * SEQS * (T - 1) * D * T


def tile_causalselfattention_pa_t_kernel(tc, h, A, out):
    nc = tc.nc
    with ExitStack() as ctx:
        keep = ctx.enter_context(tc.tile_pool(name="keep", bufs=1))
        h_stage = ctx.enter_context(tc.tile_pool(name="h_stage", bufs=ROUND))
        ha_stage = ctx.enter_context(tc.tile_pool(name="ha_stage", bufs=3))
        soft = ctx.enter_context(tc.tile_pool(name="soft", bufs=2))
        bank_psum = ctx.enter_context(tc.psum_pool(name="bank_psum", bufs=7))
        score_psum = ctx.enter_context(tc.psum_pool(name="score_psum", bufs=1))

        ctx.enter_context(tc.manual_schedule())

        identity = keep.tile([P, P], F32)
        make_identity(nc, identity[:])
        mask = keep.tile([P, P], F32)
        nc.gpsimd.memset(mask[:], 0.0)
        nc.gpsimd.affine_select(
            out=mask[:],
            in_=mask[:],
            pattern=[[-1, P]],
            compare_op=ALU.is_ge,
            fill=-NEG_INF,
            base=0,
            channel_multiplier=1,
        )
        table_in = keep.tile([P, 1], F32)
        table_out = keep.tile([P, 1], F32)
        nc.vector.memset(table_in[:], 0.0)
        nc.scalar.activation(out=table_out[:], in_=table_in[:], func=ACT.Exp)

        h_raw = keep.tile([P, GROUPS, D], BF16)
        h_words = h_raw[:].rearrange("p g d -> p (g d)").bitcast(F32)
        h_codes = keep.tile([P, GROUPS, PASSES * P], U32, align_bytes=64)
        h_scales = keep.tile([P, GROUPS, PASSES * P], U8, align_bytes=64)
        a_raw = keep.tile([P, PASSES, PASSES, PACK, K_PASS], BF16)
        a_codes = keep.tile([P, PASSES, D], U32, align_bytes=64)
        a_scales = keep.tile([P, PASSES, D], U8, align_bytes=64)
        ha_codes = keep.tile([P, GROUPS, PASSES * P], U32, align_bytes=64)
        ha_scales = keep.tile([P, GROUPS, PASSES * P], U8, align_bytes=64)
        attn = keep.tile([P, GROUPS, T], F32)

        h_rows = h.rearrange("b t d -> (b t) d").rearrange("(g p) d -> p g d", p=P)
        a_rows = A.rearrange("n (c u p v) e -> p (n c) u v e", c=PASSES, u=2, v=2)
        out_rows = out.rearrange("(g b) n t s -> (b n t) g s", b=SEQS_IN_GROUP)

        def load_h(first, last):
            nc.sync.dma_start(out=h_raw[:, first:last, :], in_=h_rows[:, first:last, :])

        def load_a(ep):
            for dp in range(PASSES):
                for u in range(2):
                    nc.sync.dma_start(
                        out=a_raw[:, ep, dp, 2 * u : 2 * u + 2, :],
                        in_=a_rows[:, dp, u, :, ep * K_PASS : (ep + 1) * K_PASS],
                    )

        load_h(0, 1)
        load_a(0)
        for grp in range(1, ROUND):
            load_h(grp, grp + 1)
        load_a(1)
        for grp in range(ROUND, 2 * ROUND):
            load_h(grp, grp + 1)
        for r in range(2, ROUNDS):
            load_h(r * ROUND, (r + 1) * ROUND)

        xt_banks = {}
        h_grouped = {}
        ha_grouped = {}
        ha_banks = {}
        a_grouped = {}
        score_banks = {}
        negated = {}
        row_min = {}
        exps = {}
        row_sum = {}
        inverse = {}

        def transpose_group(grp):
            xt_banks[grp] = bank_psum.tile([P, PACK, P], F32, name="xt_bank", tag="bank")
            for quarter in range(PACK):
                first_word = grp * WORDS + quarter * P
                nc.tensor.transpose(
                    xt_banks[grp][:, quarter, :],
                    h_words[:, first_word : first_word + P],
                    identity[:],
                )

        def copy_h(grp, on_scalar):
            if grp % 2 == 0:
                h_grouped[grp // 2] = h_stage.tile([P, 2, PASSES * P * PACK], BF16, align_bytes=64, name="h_grouped")
            pairs_out = h_grouped[grp // 2][:, grp % 2].bitcast(F32).rearrange("p (c r u) -> p c r u", c=PASSES, u=2)
            pairs_in = xt_banks[grp][:].rearrange("p (c u) r -> p c r u", u=2)
            if on_scalar:
                nc.scalar.copy(out=pairs_out, in_=pairs_in)
            else:
                nc.vector.tensor_copy(out=pairs_out, in_=pairs_in)

        def quantise_h(grp, count=1):
            groups = slice(grp, grp + count)
            halves = slice(grp % 2, grp % 2 + count)
            nc.vector.quantize_mx(
                out=h_codes[:, groups, :].rearrange("p g w -> p (g w)").bitcast(FP8X4),
                scales=h_scales[:, groups, :].rearrange("p g w -> p (g w)"),
                in_=h_grouped[grp // 2][:, halves].rearrange("p g k -> p (g k)"),
            )

        def copy_a(dp, ep):
            a_grouped[dp, ep] = keep.tile(
                [P, 2, 2, P, PACK], BF16, align_bytes=64, name="a_grouped%d%d" % (dp, ep)
            )
            for u in range(2):
                src = a_raw[:, ep, dp, :, u * 2 * P : (u + 1) * 2 * P]
                src = src.rearrange("p j (q v) -> p q j v", v=2)
                dst = a_grouped[dp, ep][:, u].rearrange("p v q j -> p q j v")
                if u == 0:
                    nc.vector.tensor_copy(out=dst, in_=src)
                else:
                    nc.scalar.copy(out=dst, in_=src)

        def quantise_a(dp, ep):
            places = slice(ep * K_PASS, (ep + 1) * K_PASS)
            nc.vector.quantize_mx(
                out=a_codes[:, dp, places].bitcast(FP8X4),
                scales=a_scales[:, dp, places],
                in_=a_grouped[dp, ep][:].rearrange("p u v q j -> p (u v q j)"),
            )

        def multiply(grp, ep):
            ha_banks[grp, ep] = bank_psum.tile([P, PACK, P], F32, name="ha_bank", tag="bank")
            for slot in range(PACK):
                places = slice((ep * PACK + slot) * P, (ep * PACK + slot + 1) * P)
                for dp in range(PASSES):
                    tokens = slice(dp * P, (dp + 1) * P)
                    nc.tensor.matmul_mx(
                        out=ha_banks[grp, ep][:, slot, :],
                        lhsT=a_codes[:, dp, places].bitcast(FP8X4),
                        lhsT_scale=a_scales[:, dp, places],
                        rhs=h_codes[:, grp, tokens].bitcast(FP8X4),
                        rhs_scale=h_scales[:, grp, tokens],
                        start=(dp == 0),
                        stop=(dp == PASSES - 1),
                    )

        def copy_ha(grp, ep, on_vector=False):
            if ep == 0 and grp % 2 == 0:
                ha_grouped[grp // 2] = ha_stage.tile([P, 2, PASSES, P, PACK], BF16, align_bytes=64, name="ha_grouped")
            words_in = ha_banks[grp, ep][:].rearrange("p slot r -> p r slot")
            if on_vector:
                nc.vector.tensor_copy(out=ha_grouped[grp // 2][:, grp % 2, ep], in_=words_in)
            else:
                nc.scalar.copy(out=ha_grouped[grp // 2][:, grp % 2, ep], in_=words_in)

        def first_matmul(grp):
            for ep in range(PASSES):
                multiply(grp, ep)
                copy_ha(grp, ep)

        def quantise_ha(grp, count=1):
            groups = slice(grp, grp + count)
            halves = slice(grp % 2, grp % 2 + count)
            nc.vector.quantize_mx(
                out=ha_codes[:, groups, :].rearrange("p g w -> p (g w)").bitcast(FP8X4),
                scales=ha_scales[:, groups, :].rearrange("p g w -> p (g w)"),
                in_=ha_grouped[grp // 2][:, halves].rearrange("p g c r slot -> p (g c r slot)"),
            )

        def second_matmul(r):
            score_banks[r] = score_psum.tile([P, ROUND, P], F32, name="score_bank")
            for i in range(ROUND):
                grp = r * ROUND + i
                for ep in range(PASSES):
                    tokens = slice(ep * P, (ep + 1) * P)
                    nc.tensor.matmul_mx(
                        out=score_banks[r][:, i, :],
                        lhsT=ha_codes[:, grp, tokens].bitcast(FP8X4),
                        lhsT_scale=ha_scales[:, grp, tokens],
                        rhs=h_codes[:, grp, tokens].bitcast(FP8X4),
                        rhs_scale=h_scales[:, grp, tokens],
                        start=(ep == 0),
                        stop=(ep == PASSES - 1),
                    )

        def take_out_scores(r):
            negated[r] = soft.tile([P, ROUND, T], F32, name="negated")
            for b in range(SEQS_IN_GROUP):
                own = slice(b * T, (b + 1) * T)
                nc.vector.tensor_tensor(
                    out=negated[r][own, :, :],
                    in0=mask[own, own].unsqueeze(1).to_broadcast([T, ROUND, T]),
                    in1=score_banks[r][own, :, own],
                    op=ALU.subtract,
                )

        def row_minima(r):
            row_min[r] = soft.tile([P, ROUND], F32, name="row_min")
            nc.vector.tensor_reduce(out=row_min[r][:], in_=negated[r][:], axis=AXIS.X, op=ALU.min)

        def exponentials(r):
            exps[r] = soft.tile([P, ROUND, T], F32, name="exps")
            row_sum[r] = soft.tile([P, ROUND], F32, name="row_sum")
            for i in range(ROUND):
                nc.scalar.activation(
                    out=exps[r][:, i, :],
                    in_=negated[r][:, i, :],
                    func=ACT.Exp,
                    scale=-1.0,
                    bias=row_min[r][:, i : i + 1],
                    accum_out=row_sum[r][:, i : i + 1],
                )

        def invert_sums(r):
            inverse[r] = soft.tile([P, ROUND], F32, name="inverse")
            nc.vector.reciprocal(out=inverse[r][:], in_=row_sum[r][:])

        def normalise_and_store(r):
            groups = slice(r * ROUND, (r + 1) * ROUND)
            nc.vector.tensor_tensor(
                out=attn[:, groups, :],
                in0=exps[r][:],
                in1=inverse[r][:].unsqueeze(2).to_broadcast([P, ROUND, T]),
                op=ALU.mult,
            )
            nc.sync.dma_start(out=out_rows[:, groups, :], in_=attn[:, groups, :])

        def quantise_ha_half(grp, ep):
            tokens = slice(ep * P, (ep + 1) * P)
            nc.vector.quantize_mx(
                out=ha_codes[:, grp, tokens].bitcast(FP8X4),
                scales=ha_scales[:, grp, tokens],
                in_=ha_grouped[grp // 2][:, grp % 2, ep].rearrange("p r slot -> p (r slot)"),
            )

        transpose_group(0)
        copy_h(0, True)
        copy_a(0, 0)
        quantise_h(0)
        copy_a(1, 0)
        quantise_a(0, 0)
        for grp in range(1, ROUND):
            transpose_group(grp)
        copy_h(1, True)
        quantise_a(1, 0)
        multiply(0, 0)
        copy_h(2, True)
        quantise_h(1)
        copy_h(3, False)
        multiply(1, 0)
        quantise_h(2)
        multiply(2, 0)
        quantise_h(3)
        multiply(3, 0)
        copy_a(0, 1)
        copy_ha(0, 0)
        copy_a(1, 1)
        quantise_a(0, 1)
        copy_ha(1, 0)
        copy_ha(2, 0, True)
        quantise_a(1, 1)
        copy_ha(3, 0)
        for grp in range(ROUND, 2 * ROUND):
            transpose_group(grp)
        for grp in range(ROUND, 2 * ROUND):
            copy_h(grp, grp == ROUND)
        multiply(0, 1)
        copy_ha(0, 1)
        multiply(1, 1)
        copy_ha(1, 1)
        for grp in range(ROUND, 2 * ROUND, 2):
            quantise_h(grp, 2)
        multiply(2, 1)
        copy_ha(2, 1)
        quantise_ha(0, 2)
        multiply(3, 1)
        copy_ha(3, 1)

        for r in range(1, ROUNDS + 2):
            multiply_turn = r < ROUNDS
            prepare = r + 1 < ROUNDS
            score = 1 <= r <= ROUNDS
            finish = r >= 2
            first = r * ROUND
            coming = first + ROUND

            if multiply_turn:
                first_matmul(first)
            if score and multiply_turn:
                quantise_ha(first - 2, 2)
            if score and not multiply_turn:
                quantise_ha_half(first - 1, 1)
            if finish:
                exponentials(r - 2)
            if prepare:
                for grp in range(coming, coming + 2):
                    transpose_group(grp)
                for grp in range(coming, coming + 2):
                    copy_h(grp, grp == coming)
            if multiply_turn:
                first_matmul(first + 1)
            if score:
                second_matmul(r - 1)
            if prepare:
                quantise_h(coming, 2)
            if multiply_turn:
                first_matmul(first + 2)
            if score:
                take_out_scores(r - 1)
            if finish:
                invert_sums(r - 2)
            if prepare:
                for grp in range(coming + 2, coming + ROUND):
                    transpose_group(grp)
                for grp in range(coming + 2, coming + ROUND):
                    copy_h(grp, grp == coming + 2)
            if multiply_turn:
                quantise_ha(first, 2)
            if score:
                row_minima(r - 1)
            if finish:
                normalise_and_store(r - 2)
            if multiply_turn:
                first_matmul(first + 3)
            if prepare:
                quantise_h(coming + 2, 2)
            if multiply_turn and not prepare:
                quantise_ha(first + 2)
                quantise_ha_half(first + 3, 0)
